import numpy as np
import ml_dtypes


def mxq(x, axis, fmt="e4m3"):
    dtype, down = {"e4m3": (ml_dtypes.float8_e4m3fn, 7), "e5m2": (ml_dtypes.float8_e5m2, 14)}[fmt]
    v = np.moveaxis(np.asarray(x, np.float32).astype(ml_dtypes.bfloat16).astype(np.float64), axis, -1)
    blocks = v.reshape(v.shape[:-1] + (-1, 32))
    amax = np.abs(blocks).max(-1, keepdims=True)
    byte = np.maximum(np.where(amax > 0, np.frexp(amax)[1] - 1 + 127, 0) - down, 1)
    scale = np.exp2(byte - 127.0)
    codes = (blocks / scale).astype(np.float32).astype(dtype).astype(np.float64)
    return np.moveaxis((codes * scale).reshape(v.shape), -1, axis)


WIDE = False


def mx_kscale(k):
    if not WIDE:
        return np.ones(k)
    levels = np.array([10, -10, 5, -5, 0])
    a = np.random.permutation(np.resize(levels, k // 512 * 4)).reshape(k // 512, 4)
    idx = np.arange(k)
    return np.exp2(a[idx // 512, idx % 128 // 32])


BF16 = ml_dtypes.bfloat16


def bf(x):
    return np.asarray(x, np.float32).astype(BF16)


def f64(x):
    return np.asarray(x).astype(np.float64)


B, IN, HID, CENT = 512, 128, 16384, 512


def setup_inputs():
    t = np.log2(mx_kscale(HID))
    a = t.max() - t
    sigmas = bf(1.0 + 0.1 * np.random.standard_normal(HID))
    c = np.random.standard_normal((HID, IN)) / np.sqrt(IN)
    c = c * np.sqrt(1.0 + a * np.log(2.0) / (f64(sigmas) ** 2 * (c * c).sum(1)))[:, None]
    return {"x": bf(np.random.standard_normal((B, IN)) / np.sqrt(IN)), "centres": bf(c), "sigmas": sigmas,
            "w1": bf(np.random.standard_normal((CENT, HID)) * 6.0 / np.sqrt(HID) * np.exp2(a)),
            "b1": bf(0.2 * np.random.standard_normal(CENT))}


def reference(x, centres, sigmas, w1, b1):
    x2 = np.sum(f64(x) * f64(x), axis=1, keepdims=True)
    c2 = np.sum(f64(centres) * f64(centres), axis=1)[None, :]
    d2 = np.maximum(x2 + c2 - 2.0 * (f64(x) @ f64(centres).T), 0.0)
    phi = np.exp(-d2 * (f64(sigmas) * f64(sigmas))[None, :])
    return np.maximum((mxq(phi, 1, "e4m3") @ mxq(f64(w1), 1, "e4m3").T) + f64(b1), 0.0)

@@ -1,0 +1,274 @@
+from contextlib import ExitStack
+
+import concourse.mybir as mybir
+from concourse.masks import make_identity
+
+F32 = mybir.dt.float32
+BF16 = mybir.dt.bfloat16
+U32 = mybir.dt.uint32
+U8 = mybir.dt.uint8
+FP8X4 = mybir.dt.float8_e4m3fn_x4
+ACT = mybir.ActivationFunctionType
+ALU = mybir.AluOpType
+
+P = 128
+B = 512
+IN = 128
+HID = 16384
+CENT = 512
+PACK = 4
+K_PASS = P * PACK
+ROUNDS = HID // K_PASS
+B_TILES = B // P
+C_TILES = CENT // P
+ROUNDS_PER_LOAD = 2
+W_LOAD = ROUNDS_PER_LOAD * K_PASS
+W_LOADS = HID // W_LOAD
+W_AHEAD = 3
+PAIRS = K_PASS // 2
+CEN_LOADS = 16
+CEN_G = HID // (2 * P)
+
+FLOPS = 2 * B * HID * (IN + CENT)
+
+
+def tile_networkprc_pa_k_kernel(tc, x, centres, sigmas, w1, b1, out):
+    nc = tc.nc
+    with ExitStack() as ctx:
+        const = ctx.enter_context(tc.tile_pool(name="const", bufs=1))
+        wload = ctx.enter_context(tc.tile_pool(name="wload", bufs=W_AHEAD + 1))
+        wgroup = ctx.enter_context(tc.tile_pool(name="wgroup", bufs=2))
+        wcodes = ctx.enter_context(tc.tile_pool(name="wcodes", bufs=5))
+        pcodes = ctx.enter_context(tc.tile_pool(name="pcodes", bufs=3))
+        cpool = ctx.enter_context(tc.tile_pool(name="cpool", bufs=4))
+        junk = ctx.enter_context(tc.tile_pool(name="junk", bufs=2))
+        dpool = ctx.enter_context(tc.tile_pool(name="dpool", bufs=4))
+        phpool = ctx.enter_context(tc.tile_pool(name="phpool", bufs=3))
+        gpool = ctx.enter_context(tc.tile_pool(name="gpool", bufs=2))
+        accps = ctx.enter_context(tc.psum_pool(name="accps", bufs=1))
+        spsum = ctx.enter_context(tc.psum_pool(name="spsum", bufs=2))
+        tpsum = ctx.enter_context(tc.psum_pool(name="tpsum", bufs=2))
+        ctx.enter_context(tc.manual_schedule())
+
+        w1_v = w1.rearrange("(ct c) j -> c ct j", c=P)
+        cen_v = centres.rearrange("(g p e) k -> p g e k", p=P, e=2)
+        out_v = out.rearrange("(p a) c -> p a c", a=B_TILES)
+
+        w_sb = {}
+        wT_ps = {}
+        wgrp = {}
+        w_codes = {}
+        w_scales = {}
+        cT_ps = {}
+        cT = {}
+        c2 = {}
+        s_ps = {}
+        d2 = {}
+        ph = {}
+        grp = {}
+        p_codes = {}
+        p_scales = {}
+
+        ident_bf = const.tile([P, P], BF16)
+        make_identity(nc, ident_bf[:])
+        ident_f32 = const.tile([P, P], F32)
+        make_identity(nc, ident_f32[:])
+        quarter = const.tile([P, P], F32)
+        nc.vector.memset(quarter[:], 0.25)
+
+        def load_w(n):
+            w_sb[n] = wload.tile([P, C_TILES, W_LOAD], BF16, name="w_sb", tag="w_sb")
+            nc.sync.dma_start(out=w_sb[n][:], in_=w1_v[:, :, n * W_LOAD : (n + 1) * W_LOAD])
+
+        def load_centres(n):
+            g_step = CEN_G // CEN_LOADS
+            nc.sync.dma_start(
+                out=cen_sb[:, n * g_step : (n + 1) * g_step, :, :],
+                in_=cen_v[:, n * g_step : (n + 1) * g_step, :, :],
+            )
+
+        def w_transposes(r):
+            n = r // ROUNDS_PER_LOAD
+            if r % ROUNDS_PER_LOAD == 0 and n + W_AHEAD < W_LOADS:
+                load_w(n + W_AHEAD)
+            first_word = (r % ROUNDS_PER_LOAD) * PAIRS
+            for h in range(2):
+                wT_ps[r, h] = tpsum.tile([P, 2, 2 * P], F32, name="wT_ps", tag="t_ps")
+                for u in range(2):
+                    for q in range(2):
+                        words = w_sb[n][:, 2 * h + q, :].bitcast(F32)
+                        nc.tensor.transpose(
+                            wT_ps[r, h][:, u, q * P : (q + 1) * P],
+                            words[:, first_word + u * P : first_word + (u + 1) * P],
+                            ident_f32[:],
+                        )
+
+        def w_copies(r):
+            wgrp[r] = wgroup.tile([P, CENT * PACK], BF16, name="wgrp", tag="wgrp", align_bytes=64)
+            words = wgrp[r][:].bitcast(F32).rearrange("p (c u) -> p c u", u=2)
+            for h in range(2):
+                nc.scalar.copy(
+                    out=words[:, h * 2 * P : (h + 1) * 2 * P, :],
+                    in_=wT_ps[r, h][:].rearrange("p u c -> p c u"),
+                )
+
+        def w_quantise(r):
+            w_codes[r] = wcodes.tile([P, CENT], U32, name="w_codes", tag="w_codes", align_bytes=64)
+            w_scales[r] = wcodes.tile([P, CENT], U8, name="w_scales", tag="w_scales", align_bytes=64)
+            nc.vector.quantize_mx(out=w_codes[r][:].bitcast(FP8X4), scales=w_scales[r][:], in_=wgrp[r][:])
+
+        def centre_tile(r, t):
+            return cen_sb[:, 2 * r + t // 2, t % 2, :]
+
+        def c_transposes(r):
+            cT_ps[r] = tpsum.tile([P, PACK, P], BF16, name="cT_ps", tag="t_ps")
+            for t in range(PACK):
+                nc.tensor.transpose(cT_ps[r][:, t, :], centre_tile(r, t), ident_bf[:])
+
+        def c_copy_and_norms(r):
+            cT[r] = cpool.tile([P, PACK, P], BF16, name="cT", tag="cT")
+            nc.scalar.copy(out=cT[r][:], in_=cT_ps[r][:])
+            c2[r] = cpool.tile([P, PACK], F32, name="c2", tag="c2")
+            squares = junk.tile([P, PACK, IN], BF16)
+            for t in range(PACK):
+                nc.scalar.activation(
+                    out=squares[:, t, :], in_=centre_tile(r, t), func=ACT.Square, accum_out=c2[r][:, t : t + 1]
+                )
+
+        def products(r, t):
+            s_ps[r, t] = spsum.tile([P, B], F32, name="s_ps", tag="s_ps")
+            nc.tensor.matmul(s_ps[r, t][:], lhsT=cT[r][:, t, :], rhs=xT2[:], start=True, stop=True)
+
+        def distances(r, t):
+            d2[r, t] = dpool.tile([P, B], F32, name="d2", tag="d2")
+            nc.vector.scalar_tensor_tensor(
+                out=d2[r, t][:],
+                in0=x2[:],
+                scalar=c2[r][:, t : t + 1],
+                in1=s_ps[r, t][:],
+                op0=ALU.add,
+                op1=ALU.subtract,
+            )
+
+        def exponentials(r, t):
+            if t == 0:
+                ph[r] = phpool.tile([P, PACK, B], BF16, name="ph", tag="ph")
+            col = PACK * r + t
+            nc.scalar.activation(out=ph[r][:, t, :], in_=d2[r, t][:], func=ACT.Exp, scale=negs2[:, col : col + 1])
+
+        def regroup(r):
+            grp[r] = gpool.tile([P, B, PACK], BF16, name="grp", tag="grp", align_bytes=64)
+            nc.vector.tensor_scalar(
+                out=grp[r][:].rearrange("p (c i) t -> p c t i", i=4),
+                in0=ph[r][:].rearrange("p t (c i) -> p c t i", i=4),
+                scalar1=1.0,
+                scalar2=None,
+                op0=ALU.min,
+            )
+
+        def p_quantise(r):
+            p_codes[r] = pcodes.tile([P, B], U32, name="p_codes", tag="p_codes", align_bytes=64)
+            p_scales[r] = pcodes.tile([P, B], U8, name="p_scales", tag="p_scales", align_bytes=64)
+            nc.vector.quantize_mx(
+                out=p_codes[r][:].bitcast(FP8X4), scales=p_scales[r][:], in_=grp[r][:].rearrange("p n t -> p (n t)")
+            )
+
+        def mx_passes(r):
+            for a in range(B_TILES):
+                nc.tensor.matmul_mx(
+                    out=acc[a][:],
+                    lhsT=p_codes[r][:, a * P : (a + 1) * P].bitcast(FP8X4),
+                    lhsT_scale=p_scales[r][:, a * P : (a + 1) * P],
+                    rhs=w_codes[r][:].bitcast(FP8X4),
+                    rhs_scale=w_scales[r][:],
+                    start=(r == 0),
+                    stop=(r == ROUNDS - 1),
+                )
+
+        x_sb = const.tile([P, B_TILES, IN], BF16)
+        nc.sync.dma_start(out=x_sb[:], in_=x.rearrange("(p a) k -> p a k", a=B_TILES))
+        cen_sb = const.tile([P, CEN_G, 2, IN], BF16)
+        load_centres(0)
+        sig_nat = const.tile([P, 2 * P], BF16)
+        nc.vector.memset(sig_nat[64:128, :], 0.0)
+        nc.sync.dma_start(out=sig_nat[0:64, :], in_=sigmas.rearrange("(g w) -> g w", w=2 * P))
+        load_w(0)
+        load_centres(1)
+        for n in range(1, W_AHEAD):
+            load_w(n)
+        for n in range(2, CEN_LOADS):
+            load_centres(n)
+        b1_bc = const.tile([P, CENT], BF16)
+        nc.sync.dma_start(out=b1_bc[:], in_=b1.partition_broadcast(P))
+
+        xT_ps = tpsum.tile([P, B_TILES, P], BF16, tag="t_ps")
+        for a in range(B_TILES):
+            nc.tensor.transpose(xT_ps[:, a, :], x_sb[:, a, :], ident_bf[:])
+        xT2 = const.tile([P, B], BF16)
+        nc.scalar.mul(out=xT2[:], in_=xT_ps[:].rearrange("p a i -> p (a i)"), mul=2.0)
+        xsq = const.tile([P, B], F32)
+        nc.vector.tensor_tensor(out=xsq[:], in0=xT2[:], in1=xT2[:], op=ALU.mult)
+
+        c_transposes(0)
+        c_copy_and_norms(0)
+
+        sigT_ps = tpsum.tile([P, P], F32, tag="t_ps")
+        nc.tensor.transpose(sigT_ps[:], sig_nat[:].bitcast(F32), ident_f32[:])
+        sigT = const.tile([P, 2 * P], BF16)
+        nc.vector.tensor_copy(out=sigT[:].bitcast(F32), in_=sigT_ps[:])
+        negs2 = const.tile([P, P], F32)
+        nc.vector.scalar_tensor_tensor(
+            out=negs2[:], in0=sigT[:, 0:P], scalar=-1.0, in1=sigT[:, 0:P], op0=ALU.mult, op1=ALU.mult
+        )
+
+        x2_ps = spsum.tile([P, B], F32, tag="s_ps")
+        nc.tensor.matmul(x2_ps[:], lhsT=quarter[:], rhs=xsq[:], start=True, stop=True)
+        x2 = const.tile([P, B], F32)
+        nc.vector.tensor_copy(out=x2[:], in_=x2_ps[:])
+
+        acc = [accps.tile([P, CENT], F32, name="acc%d" % a) for a in range(B_TILES)]
+
+        products(0, 0)
+        products(0, 1)
+        c_transposes(1)
+        c_copy_and_norms(1)
+        w_transposes(0)
+        w_copies(0)
+        w_quantise(0)
+
+        for i in range(ROUNDS + 2):
+            if i < ROUNDS:
+                distances(i, 0)
+                distances(i, 1)
+                products(i, 2)
+                products(i, 3)
+                exponentials(i, 0)
+                exponentials(i, 1)
+            if 0 <= i - 1 < ROUNDS:
+                regroup(i - 1)
+            if i + 1 < ROUNDS:
+                w_transposes(i + 1)
+                w_copies(i + 1)
+            if 0 <= i - 2:
+                mx_passes(i - 2)
+            if i + 2 < ROUNDS:
+                c_transposes(i + 2)
+            if i < ROUNDS:
+                distances(i, 2)
+                distances(i, 3)
+                exponentials(i, 2)
+                exponentials(i, 3)
+            if i + 1 < ROUNDS:
+                products(i + 1, 0)
+                products(i + 1, 1)
+                w_quantise(i + 1)
+            if 0 <= i - 1 < ROUNDS:
+                p_quantise(i - 1)
+            if i + 2 < ROUNDS:
+                c_copy_and_norms(i + 2)
+
+        res = const.tile([P, B_TILES, CENT], F32)
+        for a in range(B_TILES):
+            nc.vector.tensor_tensor(out=res[:, a, :], in0=acc[a][:], in1=b1_bc[:], op=ALU.add)
+            nc.scalar.activation(out=res[:, a, :], in_=res[:, a, :], func=ACT.Relu)
+            nc.sync.dma_start(out=out_v[:, a, :], in_=res[:, a, :])

@@ -28,6 +28,7 @@ W_AHEAD = 3
 PAIRS = K_PASS // 2
 CEN_LOADS = 16
 CEN_G = HID // (2 * P)
+REGROUP_PIECES = 4
 
 FLOPS = 2 * B * HID * (IN + CENT)
 
@@ -37,14 +38,14 @@ def tile_networkprc_pa_k_kernel(tc, x, centres, sigmas, w1, b1, out):
     with ExitStack() as ctx:
         const = ctx.enter_context(tc.tile_pool(name="const", bufs=1))
         wload = ctx.enter_context(tc.tile_pool(name="wload", bufs=W_AHEAD + 1))
-        wgroup = ctx.enter_context(tc.tile_pool(name="wgroup", bufs=2))
-        wcodes = ctx.enter_context(tc.tile_pool(name="wcodes", bufs=5))
+        wgroup = ctx.enter_context(tc.tile_pool(name="wgroup", bufs=3))
+        wcodes = ctx.enter_context(tc.tile_pool(name="wcodes", bufs=6))
         pcodes = ctx.enter_context(tc.tile_pool(name="pcodes", bufs=3))
         cpool = ctx.enter_context(tc.tile_pool(name="cpool", bufs=4))
         junk = ctx.enter_context(tc.tile_pool(name="junk", bufs=2))
         dpool = ctx.enter_context(tc.tile_pool(name="dpool", bufs=4))
         phpool = ctx.enter_context(tc.tile_pool(name="phpool", bufs=3))
-        gpool = ctx.enter_context(tc.tile_pool(name="gpool", bufs=2))
+        gpool = ctx.enter_context(tc.tile_pool(name="gpool", bufs=3))
         accps = ctx.enter_context(tc.psum_pool(name="accps", bufs=1))
         spsum = ctx.enter_context(tc.psum_pool(name="spsum", bufs=2))
         tpsum = ctx.enter_context(tc.psum_pool(name="tpsum", bufs=2))
@@ -103,14 +104,14 @@ def tile_networkprc_pa_k_kernel(tc, x, centres, sigmas, w1, b1, out):
                             ident_f32[:],
                         )
 
-        def w_copies(r):
-            wgrp[r] = wgroup.tile([P, CENT * PACK], BF16, name="wgrp", tag="wgrp", align_bytes=64)
-            words = wgrp[r][:].bitcast(F32).rearrange("p (c u) -> p c u", u=2)
-            for h in range(2):
-                nc.scalar.copy(
-                    out=words[:, h * 2 * P : (h + 1) * 2 * P, :],
-                    in_=wT_ps[r, h][:].rearrange("p u c -> p c u"),
-                )
+        def w_copy(r, h):
+            if h == 0:
+                wgrp[r] = wgroup.tile([P, CENT * PACK], BF16, name="wgrp", tag="wgrp", align_bytes=64)
+            words = wgrp[r][:].bitcast(F32).rearrange("p (c u) -> p c u", u=2)[:, h * 2 * P : (h + 1) * 2 * P, :]
+            if h == 0:
+                nc.scalar.copy(out=words, in_=wT_ps[r, h][:].rearrange("p u c -> p c u"))
+            else:
+                nc.vector.tensor_copy(out=words, in_=wT_ps[r, h][:].rearrange("p u c -> p c u"))
 
         def w_quantise(r):
             w_codes[r] = wcodes.tile([P, CENT], U32, name="w_codes", tag="w_codes", align_bytes=64)
@@ -158,13 +159,16 @@ def tile_networkprc_pa_k_kernel(tc, x, centres, sigmas, w1, b1, out):
 
         def regroup(r):
             grp[r] = gpool.tile([P, B, PACK], BF16, name="grp", tag="grp", align_bytes=64)
-            nc.vector.tensor_scalar(
-                out=grp[r][:].rearrange("p (c i) t -> p c t i", i=4),
-                in0=ph[r][:].rearrange("p t (c i) -> p c t i", i=4),
-                scalar1=1.0,
-                scalar2=None,
-                op0=ALU.min,
-            )
+            step = B // REGROUP_PIECES
+            for n in range(0, B, step):
+                nc.gpsimd.tensor_scalar(
+                    out=grp[r][:, n : n + step, :],
+                    in0=ph[r][:, :, n : n + step].rearrange("p t n -> p n t"),
+                    scalar1=1.0,
+                    scalar2=0.0,
+                    op0=ALU.min,
+                    op1=ALU.max,
+                )
 
         def p_quantise(r):
             p_codes[r] = pcodes.tile([P, B], U32, name="p_codes", tag="p_codes", align_bytes=64)
@@ -233,10 +237,10 @@ def tile_networkprc_pa_k_kernel(tc, x, centres, sigmas, w1, b1, out):
         c_transposes(1)
         c_copy_and_norms(1)
         w_transposes(0)
-        w_copies(0)
-        w_quantise(0)
+        w_copy(0, 0)
+        w_copy(0, 1)
 
-        for i in range(ROUNDS + 2):
+        for i in range(ROUNDS + 3):
             if i < ROUNDS:
                 distances(i, 0)
                 distances(i, 1)
@@ -246,26 +250,27 @@ def tile_networkprc_pa_k_kernel(tc, x, centres, sigmas, w1, b1, out):
                 exponentials(i, 1)
             if 0 <= i - 1 < ROUNDS:
                 regroup(i - 1)
-            if i + 1 < ROUNDS:
-                w_transposes(i + 1)
-                w_copies(i + 1)
-            if 0 <= i - 2:
-                mx_passes(i - 2)
+            if i < ROUNDS:
+                w_quantise(i)
+            if 0 <= i - 2 < ROUNDS:
+                p_quantise(i - 2)
             if i + 2 < ROUNDS:
                 c_transposes(i + 2)
+                c_copy_and_norms(i + 2)
+            if i + 1 < ROUNDS:
+                w_transposes(i + 1)
+                w_copy(i + 1, 0)
             if i < ROUNDS:
                 distances(i, 2)
                 distances(i, 3)
                 exponentials(i, 2)
                 exponentials(i, 3)
             if i + 1 < ROUNDS:
+                w_copy(i + 1, 1)
                 products(i + 1, 0)
                 products(i + 1, 1)
-                w_quantise(i + 1)
-            if 0 <= i - 1 < ROUNDS:
-                p_quantise(i - 1)
-            if i + 2 < ROUNDS:
-                c_copy_and_norms(i + 2)
+            if 0 <= i - 3 < ROUNDS:
+                mx_passes(i - 3)
 
         res = const.tile([P, B_TILES, CENT], F32)
         for a in range(B_TILES):

@@ -28,7 +28,7 @@ W_AHEAD = 3
 PAIRS = K_PASS // 2
 CEN_LOADS = 16
 CEN_G = HID // (2 * P)
-REGROUP_PIECES = 4
+REGROUP_PIECES = 1
 
 FLOPS = 2 * B * HID * (IN + CENT)
 

@@ -28,7 +28,7 @@ W_AHEAD = 3
 PAIRS = K_PASS // 2
 CEN_LOADS = 16
 CEN_G = HID // (2 * P)
-REGROUP_PIECES = 1
+GPSIMD_COLS = 384
 
 FLOPS = 2 * B * HID * (IN + CENT)
 
@@ -45,7 +45,7 @@ def tile_networkprc_pa_k_kernel(tc, x, centres, sigmas, w1, b1, out):
         junk = ctx.enter_context(tc.tile_pool(name="junk", bufs=2))
         dpool = ctx.enter_context(tc.tile_pool(name="dpool", bufs=4))
         phpool = ctx.enter_context(tc.tile_pool(name="phpool", bufs=3))
-        gpool = ctx.enter_context(tc.tile_pool(name="gpool", bufs=3))
+        gpool = ctx.enter_context(tc.tile_pool(name="gpool", bufs=1))
         accps = ctx.enter_context(tc.psum_pool(name="accps", bufs=1))
         spsum = ctx.enter_context(tc.psum_pool(name="spsum", bufs=2))
         tpsum = ctx.enter_context(tc.psum_pool(name="tpsum", bufs=2))
@@ -104,14 +104,14 @@ def tile_networkprc_pa_k_kernel(tc, x, centres, sigmas, w1, b1, out):
                             ident_f32[:],
                         )
 
-        def w_copy(r, h):
-            if h == 0:
-                wgrp[r] = wgroup.tile([P, CENT * PACK], BF16, name="wgrp", tag="wgrp", align_bytes=64)
-            words = wgrp[r][:].bitcast(F32).rearrange("p (c u) -> p c u", u=2)[:, h * 2 * P : (h + 1) * 2 * P, :]
-            if h == 0:
-                nc.scalar.copy(out=words, in_=wT_ps[r, h][:].rearrange("p u c -> p c u"))
-            else:
-                nc.vector.tensor_copy(out=words, in_=wT_ps[r, h][:].rearrange("p u c -> p c u"))
+        def w_copies(r):
+            wgrp[r] = wgroup.tile([P, CENT * PACK], BF16, name="wgrp", tag="wgrp", align_bytes=64)
+            words = wgrp[r][:].bitcast(F32).rearrange("p (c u) -> p c u", u=2)
+            for h in range(2):
+                nc.scalar.copy(
+                    out=words[:, h * 2 * P : (h + 1) * 2 * P, :],
+                    in_=wT_ps[r, h][:].rearrange("p u c -> p c u"),
+                )
 
         def w_quantise(r):
             w_codes[r] = wcodes.tile([P, CENT], U32, name="w_codes", tag="w_codes", align_bytes=64)
@@ -126,9 +126,11 @@ def tile_networkprc_pa_k_kernel(tc, x, centres, sigmas, w1, b1, out):
             for t in range(PACK):
                 nc.tensor.transpose(cT_ps[r][:, t, :], centre_tile(r, t), ident_bf[:])
 
-        def c_copy_and_norms(r):
+        def c_copy(r):
             cT[r] = cpool.tile([P, PACK, P], BF16, name="cT", tag="cT")
-            nc.scalar.copy(out=cT[r][:], in_=cT_ps[r][:])
+            nc.vector.tensor_copy(out=cT[r][:], in_=cT_ps[r][:])
+
+        def c_norms(r):
             c2[r] = cpool.tile([P, PACK], F32, name="c2", tag="c2")
             squares = junk.tile([P, PACK, IN], BF16)
             for t in range(PACK):
@@ -159,16 +161,21 @@ def tile_networkprc_pa_k_kernel(tc, x, centres, sigmas, w1, b1, out):
 
         def regroup(r):
             grp[r] = gpool.tile([P, B, PACK], BF16, name="grp", tag="grp", align_bytes=64)
-            step = B // REGROUP_PIECES
-            for n in range(0, B, step):
-                nc.gpsimd.tensor_scalar(
-                    out=grp[r][:, n : n + step, :],
-                    in0=ph[r][:, :, n : n + step].rearrange("p t n -> p n t"),
-                    scalar1=1.0,
-                    scalar2=0.0,
-                    op0=ALU.min,
-                    op1=ALU.max,
-                )
+            nc.vector.tensor_scalar(
+                out=grp[r][:, GPSIMD_COLS:B, :].rearrange("p (c i) t -> p c t i", i=4),
+                in0=ph[r][:, :, GPSIMD_COLS:B].rearrange("p t (c i) -> p c t i", i=4),
+                scalar1=1.0,
+                scalar2=None,
+                op0=ALU.min,
+            )
+            nc.gpsimd.tensor_scalar(
+                out=grp[r][:, 0:GPSIMD_COLS, :],
+                in0=ph[r][:, :, 0:GPSIMD_COLS].rearrange("p t n -> p n t"),
+                scalar1=1.0,
+                scalar2=0.0,
+                op0=ALU.min,
+                op1=ALU.max,
+            )
 
         def p_quantise(r):
             p_codes[r] = pcodes.tile([P, B], U32, name="p_codes", tag="p_codes", align_bytes=64)
@@ -214,7 +221,8 @@ def tile_networkprc_pa_k_kernel(tc, x, centres, sigmas, w1, b1, out):
         nc.vector.tensor_tensor(out=xsq[:], in0=xT2[:], in1=xT2[:], op=ALU.mult)
 
         c_transposes(0)
-        c_copy_and_norms(0)
+        c_copy(0)
+        c_norms(0)
 
         sigT_ps = tpsum.tile([P, P], F32, tag="t_ps")
         nc.tensor.transpose(sigT_ps[:], sig_nat[:].bitcast(F32), ident_f32[:])
@@ -235,10 +243,10 @@ def tile_networkprc_pa_k_kernel(tc, x, centres, sigmas, w1, b1, out):
         products(0, 0)
         products(0, 1)
         c_transposes(1)
-        c_copy_and_norms(1)
+        c_copy(1)
+        c_norms(1)
         w_transposes(0)
-        w_copy(0, 0)
-        w_copy(0, 1)
+        w_copies(0)
 
         for i in range(ROUNDS + 3):
             if i < ROUNDS:
@@ -248,25 +256,25 @@ def tile_networkprc_pa_k_kernel(tc, x, centres, sigmas, w1, b1, out):
                 products(i, 3)
                 exponentials(i, 0)
                 exponentials(i, 1)
-            if 0 <= i - 1 < ROUNDS:
-                regroup(i - 1)
-            if i < ROUNDS:
                 w_quantise(i)
             if 0 <= i - 2 < ROUNDS:
                 p_quantise(i - 2)
-            if i + 2 < ROUNDS:
-                c_transposes(i + 2)
-                c_copy_and_norms(i + 2)
+            if 0 <= i - 1 < ROUNDS:
+                regroup(i - 1)
             if i + 1 < ROUNDS:
                 w_transposes(i + 1)
-                w_copy(i + 1, 0)
+                w_copies(i + 1)
+            if i + 2 < ROUNDS:
+                c_transposes(i + 2)
             if i < ROUNDS:
                 distances(i, 2)
                 distances(i, 3)
                 exponentials(i, 2)
                 exponentials(i, 3)
+            if i + 2 < ROUNDS:
+                c_copy(i + 2)
+                c_norms(i + 2)
             if i + 1 < ROUNDS:
-                w_copy(i + 1, 1)
                 products(i + 1, 0)
                 products(i + 1, 1)
             if 0 <= i - 3 < ROUNDS:

from contextlib import ExitStack

import concourse.mybir as mybir
from concourse.masks import make_identity

F32 = mybir.dt.float32
BF16 = mybir.dt.bfloat16
U32 = mybir.dt.uint32
U8 = mybir.dt.uint8
FP8X4 = mybir.dt.float8_e4m3fn_x4
ACT = mybir.ActivationFunctionType
ALU = mybir.AluOpType

P = 128
B = 512
IN = 128
HID = 16384
CENT = 512
PACK = 4
K_PASS = P * PACK
ROUNDS = HID // K_PASS
B_TILES = B // P
C_TILES = CENT // P
ROUNDS_PER_LOAD = 2
W_LOAD = ROUNDS_PER_LOAD * K_PASS
W_LOADS = HID // W_LOAD
W_AHEAD = 3
PAIRS = K_PASS // 2
CEN_LOADS = 16
CEN_G = HID // (2 * P)
GPSIMD_COLS = 384

FLOPS = 2 * B * HID * (IN + CENT)


def tile_networkprc_pa_k_kernel(tc, x, centres, sigmas, w1, b1, out):
    nc = tc.nc
    with ExitStack() as ctx:
        const = ctx.enter_context(tc.tile_pool(name="const", bufs=1))
        wload = ctx.enter_context(tc.tile_pool(name="wload", bufs=W_AHEAD + 1))
        wgroup = ctx.enter_context(tc.tile_pool(name="wgroup", bufs=3))
        wcodes = ctx.enter_context(tc.tile_pool(name="wcodes", bufs=6))
        pcodes = ctx.enter_context(tc.tile_pool(name="pcodes", bufs=3))
        cpool = ctx.enter_context(tc.tile_pool(name="cpool", bufs=4))
        junk = ctx.enter_context(tc.tile_pool(name="junk", bufs=2))
        dpool = ctx.enter_context(tc.tile_pool(name="dpool", bufs=4))
        phpool = ctx.enter_context(tc.tile_pool(name="phpool", bufs=3))
        gpool = ctx.enter_context(tc.tile_pool(name="gpool", bufs=1))
        accps = ctx.enter_context(tc.psum_pool(name="accps", bufs=1))
        spsum = ctx.enter_context(tc.psum_pool(name="spsum", bufs=2))
        tpsum = ctx.enter_context(tc.psum_pool(name="tpsum", bufs=2))
        ctx.enter_context(tc.manual_schedule())

        w1_v = w1.rearrange("(ct c) j -> c ct j", c=P)
        cen_v = centres.rearrange("(g p e) k -> p g e k", p=P, e=2)
        out_v = out.rearrange("(p a) c -> p a c", a=B_TILES)

        w_sb = {}
        wT_ps = {}
        wgrp = {}
        w_codes = {}
        w_scales = {}
        cT_ps = {}
        cT = {}
        c2 = {}
        s_ps = {}
        d2 = {}
        ph = {}
        grp = {}
        p_codes = {}
        p_scales = {}

        ident_bf = const.tile([P, P], BF16)
        make_identity(nc, ident_bf[:])
        ident_f32 = const.tile([P, P], F32)
        make_identity(nc, ident_f32[:])
        quarter = const.tile([P, P], F32)
        nc.vector.memset(quarter[:], 0.25)

        def load_w(n):
            w_sb[n] = wload.tile([P, C_TILES, W_LOAD], BF16, name="w_sb", tag="w_sb")
            nc.sync.dma_start(out=w_sb[n][:], in_=w1_v[:, :, n * W_LOAD : (n + 1) * W_LOAD])

        def load_centres(n):
            g_step = CEN_G // CEN_LOADS
            nc.sync.dma_start(
                out=cen_sb[:, n * g_step : (n + 1) * g_step, :, :],
                in_=cen_v[:, n * g_step : (n + 1) * g_step, :, :],
            )

        def w_transposes(r):
            n = r // ROUNDS_PER_LOAD
            if r % ROUNDS_PER_LOAD == 0 and n + W_AHEAD < W_LOADS:
                load_w(n + W_AHEAD)
            first_word = (r % ROUNDS_PER_LOAD) * PAIRS
            for h in range(2):
                wT_ps[r, h] = tpsum.tile([P, 2, 2 * P], F32, name="wT_ps", tag="t_ps")
                for u in range(2):
                    for q in range(2):
                        words = w_sb[n][:, 2 * h + q, :].bitcast(F32)
                        nc.tensor.transpose(
                            wT_ps[r, h][:, u, q * P : (q + 1) * P],
                            words[:, first_word + u * P : first_word + (u + 1) * P],
                            ident_f32[:],
                        )

        def w_copies(r):
            wgrp[r] = wgroup.tile([P, CENT * PACK], BF16, name="wgrp", tag="wgrp", align_bytes=64)
            words = wgrp[r][:].bitcast(F32).rearrange("p (c u) -> p c u", u=2)
            for h in range(2):
                nc.scalar.copy(
                    out=words[:, h * 2 * P : (h + 1) * 2 * P, :],
                    in_=wT_ps[r, h][:].rearrange("p u c -> p c u"),
                )

        def w_quantise(r):
            w_codes[r] = wcodes.tile([P, CENT], U32, name="w_codes", tag="w_codes", align_bytes=64)
            w_scales[r] = wcodes.tile([P, CENT], U8, name="w_scales", tag="w_scales", align_bytes=64)
            nc.vector.quantize_mx(out=w_codes[r][:].bitcast(FP8X4), scales=w_scales[r][:], in_=wgrp[r][:])

        def centre_tile(r, t):
            return cen_sb[:, 2 * r + t // 2, t % 2, :]

        def c_transposes(r):
            cT_ps[r] = tpsum.tile([P, PACK, P], BF16, name="cT_ps", tag="t_ps")
            for t in range(PACK):
                nc.tensor.transpose(cT_ps[r][:, t, :], centre_tile(r, t), ident_bf[:])

        def c_copy(r):
            cT[r] = cpool.tile([P, PACK, P], BF16, name="cT", tag="cT")
            nc.vector.tensor_copy(out=cT[r][:], in_=cT_ps[r][:])

        def c_norms(r):
            c2[r] = cpool.tile([P, PACK], F32, name="c2", tag="c2")
            squares = junk.tile([P, PACK, IN], BF16)
            for t in range(PACK):
                nc.scalar.activation(
                    out=squares[:, t, :], in_=centre_tile(r, t), func=ACT.Square, accum_out=c2[r][:, t : t + 1]
                )

        def products(r, t):
            s_ps[r, t] = spsum.tile([P, B], F32, name="s_ps", tag="s_ps")
            nc.tensor.matmul(s_ps[r, t][:], lhsT=cT[r][:, t, :], rhs=xT2[:], start=True, stop=True)

        def distances(r, t):
            d2[r, t] = dpool.tile([P, B], F32, name="d2", tag="d2")
            nc.vector.scalar_tensor_tensor(
                out=d2[r, t][:],
                in0=x2[:],
                scalar=c2[r][:, t : t + 1],
                in1=s_ps[r, t][:],
                op0=ALU.add,
                op1=ALU.subtract,
            )

        def exponentials(r, t):
            if t == 0:
                ph[r] = phpool.tile([P, PACK, B], BF16, name="ph", tag="ph")
            col = PACK * r + t
            nc.scalar.activation(out=ph[r][:, t, :], in_=d2[r, t][:], func=ACT.Exp, scale=negs2[:, col : col + 1])

        def regroup(r):
            grp[r] = gpool.tile([P, B, PACK], BF16, name="grp", tag="grp", align_bytes=64)
            nc.vector.tensor_scalar(
                out=grp[r][:, GPSIMD_COLS:B, :].rearrange("p (c i) t -> p c t i", i=4),
                in0=ph[r][:, :, GPSIMD_COLS:B].rearrange("p t (c i) -> p c t i", i=4),
                scalar1=1.0,
                scalar2=None,
                op0=ALU.min,
            )
            nc.gpsimd.tensor_scalar(
                out=grp[r][:, 0:GPSIMD_COLS, :],
                in0=ph[r][:, :, 0:GPSIMD_COLS].rearrange("p t n -> p n t"),
                scalar1=1.0,
                scalar2=0.0,
                op0=ALU.min,
                op1=ALU.max,
            )

        def p_quantise(r):
            p_codes[r] = pcodes.tile([P, B], U32, name="p_codes", tag="p_codes", align_bytes=64)
            p_scales[r] = pcodes.tile([P, B], U8, name="p_scales", tag="p_scales", align_bytes=64)
            nc.vector.quantize_mx(
                out=p_codes[r][:].bitcast(FP8X4), scales=p_scales[r][:], in_=grp[r][:].rearrange("p n t -> p (n t)")
            )

        def mx_passes(r):
            for a in range(B_TILES):
                nc.tensor.matmul_mx(
                    out=acc[a][:],
                    lhsT=p_codes[r][:, a * P : (a + 1) * P].bitcast(FP8X4),
                    lhsT_scale=p_scales[r][:, a * P : (a + 1) * P],
                    rhs=w_codes[r][:].bitcast(FP8X4),
                    rhs_scale=w_scales[r][:],
                    start=(r == 0),
                    stop=(r == ROUNDS - 1),
                )

        x_sb = const.tile([P, B_TILES, IN], BF16)
        nc.sync.dma_start(out=x_sb[:], in_=x.rearrange("(p a) k -> p a k", a=B_TILES))
        cen_sb = const.tile([P, CEN_G, 2, IN], BF16)
        load_centres(0)
        sig_nat = const.tile([P, 2 * P], BF16)
        nc.vector.memset(sig_nat[64:128, :], 0.0)
        nc.sync.dma_start(out=sig_nat[0:64, :], in_=sigmas.rearrange("(g w) -> g w", w=2 * P))
        load_w(0)
        load_centres(1)
        for n in range(1, W_AHEAD):
            load_w(n)
        for n in range(2, CEN_LOADS):
            load_centres(n)
        b1_bc = const.tile([P, CENT], BF16)
        nc.sync.dma_start(out=b1_bc[:], in_=b1.partition_broadcast(P))

        xT_ps = tpsum.tile([P, B_TILES, P], BF16, tag="t_ps")
        for a in range(B_TILES):
            nc.tensor.transpose(xT_ps[:, a, :], x_sb[:, a, :], ident_bf[:])
        xT2 = const.tile([P, B], BF16)
        nc.scalar.mul(out=xT2[:], in_=xT_ps[:].rearrange("p a i -> p (a i)"), mul=2.0)
        xsq = const.tile([P, B], F32)
        nc.vector.tensor_tensor(out=xsq[:], in0=xT2[:], in1=xT2[:], op=ALU.mult)

        c_transposes(0)
        c_copy(0)
        c_norms(0)

        sigT_ps = tpsum.tile([P, P], F32, tag="t_ps")
        nc.tensor.transpose(sigT_ps[:], sig_nat[:].bitcast(F32), ident_f32[:])
        sigT = const.tile([P, 2 * P], BF16)
        nc.vector.tensor_copy(out=sigT[:].bitcast(F32), in_=sigT_ps[:])
        negs2 = const.tile([P, P], F32)
        nc.vector.scalar_tensor_tensor(
            out=negs2[:], in0=sigT[:, 0:P], scalar=-1.0, in1=sigT[:, 0:P], op0=ALU.mult, op1=ALU.mult
        )

        x2_ps = spsum.tile([P, B], F32, tag="s_ps")
        nc.tensor.matmul(x2_ps[:], lhsT=quarter[:], rhs=xsq[:], start=True, stop=True)
        x2 = const.tile([P, B], F32)
        nc.vector.tensor_copy(out=x2[:], in_=x2_ps[:])

        acc = [accps.tile([P, CENT], F32, name="acc%d" % a) for a in range(B_TILES)]

        products(0, 0)
        products(0, 1)
        c_transposes(1)
        c_copy(1)
        c_norms(1)
        w_transposes(0)
        w_copies(0)

        for i in range(ROUNDS + 3):
            if i < ROUNDS:
                distances(i, 0)
                distances(i, 1)
                products(i, 2)
                products(i, 3)
                exponentials(i, 0)
                exponentials(i, 1)
                w_quantise(i)
            if 0 <= i - 2 < ROUNDS:
                p_quantise(i - 2)
            if 0 <= i - 1 < ROUNDS:
                regroup(i - 1)
            if i + 1 < ROUNDS:
                w_transposes(i + 1)
                w_copies(i + 1)
            if i + 2 < ROUNDS:
                c_transposes(i + 2)
            if i < ROUNDS:
                distances(i, 2)
                distances(i, 3)
                exponentials(i, 2)
                exponentials(i, 3)
            if i + 2 < ROUNDS:
                c_copy(i + 2)
                c_norms(i + 2)
            if i + 1 < ROUNDS:
                products(i + 1, 0)
                products(i + 1, 1)
            if 0 <= i - 3 < ROUNDS:
                mx_passes(i - 3)

        res = const.tile([P, B_TILES, CENT], F32)
        for a in range(B_TILES):
            nc.vector.tensor_tensor(out=res[:, a, :], in0=acc[a][:], in1=b1_bc[:], op=ALU.add)
            nc.scalar.activation(out=res[:, a, :], in_=res[:, a, :], func=ACT.Relu)
            nc.sync.dma_start(out=out_v[:, a, :], in_=res[:, a, :])
